import numpy as np
import ml_dtypes


def mxq(x, axis, fmt="e4m3"):
    dtype, down = {"e4m3": (ml_dtypes.float8_e4m3fn, 7), "e5m2": (ml_dtypes.float8_e5m2, 14)}[fmt]
    v = np.moveaxis(np.asarray(x, np.float32).astype(ml_dtypes.bfloat16).astype(np.float64), axis, -1)
    blocks = v.reshape(v.shape[:-1] + (-1, 32))
    amax = np.abs(blocks).max(-1, keepdims=True)
    byte = np.maximum(np.where(amax > 0, np.frexp(amax)[1] - 1 + 127, 0) - down, 1)
    scale = np.exp2(byte - 127.0)
    codes = (blocks / scale).astype(np.float32).astype(dtype).astype(np.float64)
    return np.moveaxis((codes * scale).reshape(v.shape), -1, axis)


WIDE = False


def mx_kscale(k):
    if not WIDE:
        return np.ones(k)
    levels = np.array([30, -30])
    if k % 512:
        return np.exp2(np.random.permutation(np.resize(levels, k // 32))).repeat(32)
    a = np.empty((k // 512, 16))
    for p in range(k // 512):
        a[p, :8] = np.random.permutation(np.resize(levels, 8))
        for g in range(8):
            far = levels[np.abs(levels - a[p, g]) >= 10]
            a[p, g + 8] = far[np.random.randint(len(far))]
    return np.exp2(a.ravel()).repeat(32)


BF16 = ml_dtypes.bfloat16


def bf(x):
    return np.asarray(x, np.float32).astype(BF16)


def f64(x):
    return np.asarray(x).astype(np.float64)


B, S, HID, NH, DH = 4, 256, 1024, 16, 64
DQ = NH * DH


def setup_inputs():
    s = mx_kscale(DQ)
    y = np.random.standard_normal((B, S, DQ)) * 0.3 * s
    h = np.ascontiguousarray(y.reshape(B, NH, S, DH).transpose(0, 2, 1, 3))
    return {"h_attn": bf(h),
            "Wo": bf(np.random.standard_normal((DQ, HID)) * 1.5 / np.sqrt(DQ) / s[:, None]),
            "bo": bf(np.random.standard_normal(HID) * 0.3)}


def reference(h_attn, Wo, bo):
    y = f64(h_attn).transpose(0, 2, 1, 3).reshape(B, -1, DQ)
    return (mxq(y, 2, "e5m2") @ mxq(f64(Wo), 0, "e5m2")) + f64(bo)

@@ -1,0 +1,207 @@
+from contextlib import ExitStack
+
+import concourse.mybir as mybir
+from concourse.masks import make_identity
+
+F32 = mybir.dt.float32
+BF16 = mybir.dt.bfloat16
+U32 = mybir.dt.uint32
+U8 = mybir.dt.uint8
+E5M2X4 = mybir.dt.float8_e5m2_x4
+ADD = mybir.AluOpType.add
+
+FLOPS = 2 * 1024 * 1024 * 1024
+
+P = 128
+VS = [[336,336],[336,336]]
+RL_ENGINE = "VVVVSSSS"
+EV_ENGINE = "SSSSSSSS"
+MANUAL = True
+ORDER = """
+ms ident perm bm0 bm1 bc0 bc1 wiV00 wiS00 wiS01 wiV01 wq00 wq01 rl0 rl1 t0_0 t0_1 rl2 t0_2 t0_3 t1_0 rl3 t1_1
+ev0 t1_2 t1_3 t2_0 t2_1 t2_2 t2_3 ev1 t3_0 t3_1 yq0 t3_2 t3_3 wiV10 wiS10 mx000 mx010 yq1 ev2 wq10 mx100 ev3
+mx110 yq2 mx001 wiS11 wiV11 mx101 mx200 mx201 rl4 mx210 fa00 rl5 fa10 st00 t4_0 t4_1 t4_2 t4_3 rl6 fa20 t5_0
+t5_1 st10 t5_2 t5_3 ev4 yq3 t6_0 st20 t6_1 t6_2 t6_3 wq11 ev5 mx300 mx301 yq4 ev6 mx011 fa30 mx111 rl7 mx211
+fa01 st30 mx310 mx311 fa11 st01 mx400 mx401 fa21 st11 mx410 mx411 fa31 st21 t7_0 t7_1 t7_2 t7_3 fa40 st31 ev7
+fa41 st40 yq5 st41 yq6 mx500 yq7 mx501 mx510 fa50 mx511 mx600 fa51 st50 mx601 mx610 fa60 st51 mx611 mx700 fa61
+st60 mx701 mx710 fa70 st61 mx711 fa71 st70 st71
+"""
+
+
+def tile_reasoningmultiheadattention_pb_kernel(tc, h_attn, Wo, bo, out):
+    nc = tc.nc
+    with ExitStack() as ctx:
+        keep = ctx.enter_context(tc.tile_pool(name="keep", bufs=1))
+        psum = ctx.enter_context(tc.psum_pool(name="psum", bufs=8))
+        if MANUAL:
+            ctx.enter_context(tc.manual_schedule())
+
+        h_flat = h_attn.rearrange("b (q j) h d -> (b q) j (h d)", j=8)
+        w_view = Wo.rearrange("(g p j) n -> g p j n", g=2, j=4)
+        out_view = out.rearrange("b (m r) n -> m r b n", r=32)
+
+        brow = keep.tile([P, 1024], BF16, name="brow")
+        ones = keep.tile([P, P], BF16, name="ones")
+        w_raw = [keep.tile([P, 4, 1024], BF16, name="w_raw%d" % g) for g in range(2)]
+        x_raw = [keep.tile([P, 8, 512], BF16, name="x_raw%d" % c) for c in range(2)]
+        ident = keep.tile([P, P], F32, name="ident")
+        perm = keep.tile([P, P], F32, name="perm")
+        bias_sb = keep.tile([P, 1024], F32, name="bias_sb")
+        w_codes = keep.tile([P, 2, 1024], U32, name="w_codes", align_bytes=64)
+        w_scales = keep.tile([P, 2, 1024], U8, name="w_scales", align_bytes=64)
+        w_grp = [[keep.tile([P, 512, 4], BF16, name="w_grp%d%d" % (g, h), align_bytes=64) for h in range(2)] for g in range(2)]
+        z = [keep.tile([P, 8, 2, P], F32, name="z%d" % c) for c in range(2)]
+        y_codes = [keep.tile([P, 256], U32, name="y_codes%d" % m, align_bytes=64) for m in range(8)]
+        y_scales = [keep.tile([P, 256], U8, name="y_scales%d" % m, align_bytes=64) for m in range(8)]
+        y_grp = [keep.tile([P, 1024], BF16, name="y_grp%d" % m, align_bytes=64) for m in range(8)]
+        res = [keep.tile([P, 1024], F32, name="res%d" % m) for m in range(8)]
+        banks = {}
+
+        nc.sync.dma_start(out=w_raw[0][:], in_=w_view[0])
+        nc.sync.dma_start(out=x_raw[0][:], in_=h_flat[:, :, 0:512])
+        nc.sync.dma_start(out=w_raw[1][:], in_=w_view[1])
+        nc.sync.dma_start(out=x_raw[1][:], in_=h_flat[:, :, 512:1024])
+
+        def copy_on(engine, dst, src):
+            if engine == "V":
+                nc.vector.tensor_copy(out=dst, in_=src)
+            else:
+                nc.scalar.copy(out=dst, in_=src)
+
+        def op_ms():
+            nc.vector.memset(brow[:], 0.0)
+            nc.vector.memset(ones[:], 1.0)
+            nc.scalar.dma_start(out=brow[0:1, :], in_=bo.rearrange("(o n) -> o n", o=1))
+
+        def op_ident():
+            make_identity(nc, ident[:])
+
+        def op_perm():
+            nc.vector.tensor_copy(
+                out=perm[:].rearrange("p (g t b) -> p g t b", g=2, t=16, b=4),
+                in_=ident[:].rearrange("p (b t g) -> p g t b", b=4, t=16, g=2),
+            )
+
+        def op_bm(h):
+            banks["b%d" % h] = psum.tile([P, 512], F32, name="bps%d" % h, tag="bank")
+            nc.tensor.matmul(out=banks["b%d" % h][:], lhsT=ones[:], rhs=brow[:, h * 512 : (h + 1) * 512], start=True, stop=True)
+
+        def op_bc(h):
+            nc.scalar.copy(out=bias_sb[:, h * 512 : (h + 1) * 512], in_=banks["b%d" % h][:])
+
+        def op_wi(engine, g, h):
+            src = w_raw[g][:, :, h * 512 : (h + 1) * 512].rearrange("p j n -> p n j")
+            cut = VS[g][h]
+            if engine == "V":
+                copy_on("V", w_grp[g][h][:, 0:cut, :], src[:, 0:cut, :])
+            else:
+                copy_on("S", w_grp[g][h][:, cut:512, :], src[:, cut:512, :])
+
+        def op_wq(g, h):
+            cols = slice(h * 512, (h + 1) * 512)
+            nc.vector.quantize_mx(
+                out=w_codes[:, g, cols].bitcast(E5M2X4),
+                scales=w_scales[:, g, cols],
+                in_=w_grp[g][h][:].rearrange("p n j -> p (n j)"),
+            )
+
+        def op_rl(m):
+            c, l = divmod(m, 4)
+            xw = x_raw[c][:].rearrange("p j e -> p (j e)").bitcast(F32)
+            xw = xw.rearrange("p (j h q u) -> p h u j q", j=8, h=8, q=16, u=2)
+            copy_on(
+                RL_ENGINE[m],
+                z[c][:, 2 * l : 2 * l + 2, :, :].rearrange("p h u (j q) -> p h u j q", j=8),
+                xw[:, 2 * l : 2 * l + 2, :, :, :],
+            )
+
+        def op_t(m, i):
+            c, l = divmod(m, 4)
+            a, u = divmod(i, 2)
+            if i == 0:
+                banks["t%d" % m] = psum.tile([P, 2, 2, 2, 64], F32, name="tp%d" % m, tag="bank")
+            nc.tensor.transpose(
+                banks["t%d" % m][:, :, u, a, :],
+                z[c][:, 2 * l + a, u, :],
+                perm[:].rearrange("p (g c) -> p g c", g=2),
+            )
+
+        def op_ev(m):
+            copy_on(
+                EV_ENGINE[m],
+                y_grp[m][:].bitcast(F32).rearrange("p (g c u) -> p g c u", g=2, c=P, u=2),
+                banks["t%d" % m][:].rearrange("p g u a c -> p g (a c) u"),
+            )
+
+        def op_yq(m):
+            nc.vector.quantize_mx(out=y_codes[m][:].bitcast(E5M2X4), scales=y_scales[m][:], in_=y_grp[m][:])
+
+        def op_mx(m, h, g):
+            if g == 0:
+                banks["a%d%d" % (m, h)] = psum.tile([P, 512], F32, name="acc%d%d" % (m, h), tag="bank")
+            cols = slice(h * 512, (h + 1) * 512)
+            rows = slice(g * P, (g + 1) * P)
+            nc.tensor.matmul_mx(
+                out=banks["a%d%d" % (m, h)][:],
+                lhsT=y_codes[m][:, rows].bitcast(E5M2X4),
+                lhsT_scale=y_scales[m][:, rows],
+                rhs=w_codes[:, g, cols].bitcast(E5M2X4),
+                rhs_scale=w_scales[:, g, cols],
+                start=(g == 0),
+                stop=(g == 1),
+            )
+
+        def op_fa(m, h):
+            cols = slice(h * 512, (h + 1) * 512)
+            nc.vector.tensor_tensor(out=res[m][:, cols], in0=banks["a%d%d" % (m, h)][:], in1=bias_sb[:, cols], op=ADD)
+
+        def op_fe(m, h):
+            cols = slice(h * 512, (h + 1) * 512)
+            nc.scalar.copy(out=res[m][:, cols], in_=banks["a%d%d" % (m, h)][:])
+
+        def op_fg(m, h):
+            cols = slice(h * 512, (h + 1) * 512)
+            nc.gpsimd.tensor_tensor(out=res[m][:, cols], in0=res[m][:, cols], in1=bias_sb[:, cols], op=ADD)
+
+        def op_st(m, h):
+            cols = slice(h * 512, (h + 1) * 512)
+            nc.sync.dma_start(out=out_view[m][:, :, cols], in_=res[m][:, cols])
+
+        for name in ORDER.split():
+            d = [int(ch) for ch in name if ch in "0123456789"]
+            if name == "ms":
+                op_ms()
+            elif name == "ident":
+                op_ident()
+            elif name == "perm":
+                op_perm()
+            elif name.startswith("bm"):
+                op_bm(d[0])
+            elif name.startswith("bc"):
+                op_bc(d[0])
+            elif name.startswith("wiV"):
+                op_wi("V", d[0], d[1])
+            elif name.startswith("wiS"):
+                op_wi("S", d[0], d[1])
+            elif name.startswith("wq"):
+                op_wq(d[0], d[1])
+            elif name.startswith("rl"):
+                op_rl(d[0])
+            elif name.startswith("t"):
+                op_t(d[0], d[1])
+            elif name.startswith("ev"):
+                op_ev(d[0])
+            elif name.startswith("yq"):
+                op_yq(d[0])
+            elif name.startswith("mx"):
+                op_mx(d[0], d[1], d[2])
+            elif name.startswith("fa"):
+                op_fa(d[0], d[1])
+            elif name.startswith("fe"):
+                op_fe(d[0], d[1])
+            elif name.startswith("fg"):
+                op_fg(d[0], d[1])
+            elif name.startswith("st"):
+                op_st(d[0], d[1])
+            else:
+                assert False, name

@@ -13,18 +13,18 @@ ADD = mybir.AluOpType.add
 FLOPS = 2 * 1024 * 1024 * 1024
 
 P = 128
-VS = [[336,336],[336,336]]
-RL_ENGINE = "VVVVSSSS"
+VS = [[336,336],[336,176]]
+RL_ENGINE = "VVSSSSSS"
 EV_ENGINE = "SSSSSSSS"
 MANUAL = True
 ORDER = """
-ms ident perm bm0 bm1 bc0 bc1 wiV00 wiS00 wiS01 wiV01 wq00 wq01 rl0 rl1 t0_0 t0_1 rl2 t0_2 t0_3 t1_0 rl3 t1_1
-ev0 t1_2 t1_3 t2_0 t2_1 t2_2 t2_3 ev1 t3_0 t3_1 yq0 t3_2 t3_3 wiV10 wiS10 mx000 mx010 yq1 ev2 wq10 mx100 ev3
-mx110 yq2 mx001 wiS11 wiV11 mx101 mx200 mx201 rl4 mx210 fa00 rl5 fa10 st00 t4_0 t4_1 t4_2 t4_3 rl6 fa20 t5_0
-t5_1 st10 t5_2 t5_3 ev4 yq3 t6_0 st20 t6_1 t6_2 t6_3 wq11 ev5 mx300 mx301 yq4 ev6 mx011 fa30 mx111 rl7 mx211
-fa01 st30 mx310 mx311 fa11 st01 mx400 mx401 fa21 st11 mx410 mx411 fa31 st21 t7_0 t7_1 t7_2 t7_3 fa40 st31 ev7
-fa41 st40 yq5 st41 yq6 mx500 yq7 mx501 mx510 fa50 mx511 mx600 fa51 st50 mx601 mx610 fa60 st51 mx611 mx700 fa61
-st60 mx701 mx710 fa70 st61 mx711 fa71 st70 st71
+ident perm wiS00 wiV01 bm0 bm1 wiV00 wiS01 wq00 bc wq01 rl2 rl0 rl1 rl3 t0_0 t0_1 t0_2 t0_3 t1_0 t1_1 ev0 t1_2
+t1_3 t2_0 wiV10 t2_1 t2_2 t2_3 wiS10 t3_0 t3_1 t3_2 t3_3 yq0 ev1 wq10 mx000 ev2 yq1 mx001 wiV11 ev3 mx100
+mx101 yq2 wiS11 yq3 mx200 fa00 mx201 mx300 fa10 mx010 st00 mx301 fa20 rl4 mx110 st10 mx310 wq11 rl5 mx210 st20
+t4_0 t4_1 fa30 rl7 t4_2 t4_3 mx011 ev4 mx111 st30 fa01 mx211 yq4 t5_0 st01 t5_1 t5_2 t5_3 fa11 ev5 mx311 mx400
+fa31 st11 rl6 mx401 mx410 yq5 st31 mx411 fa40 t6_0 t6_1 t6_2 t6_3 fa21 st40 ev6 mx500 mx510 fa41 st21 mx501
+mx511 yq6 st41 t7_0 fa50 t7_1 t7_2 t7_3 ev7 mx600 fa51 st50 mx601 mx610 yq7 st51 mx611 fa60 mx700 mx710 fa61
+mx711 st60 mx701 st61 fa70 fa71 st70 st71
 """
 
 
@@ -46,7 +46,7 @@ def tile_reasoningmultiheadattention_pb_kernel(tc, h_attn, Wo, bo, out):
         x_raw = [keep.tile([P, 8, 512], BF16, name="x_raw%d" % c) for c in range(2)]
         ident = keep.tile([P, P], F32, name="ident")
         perm = keep.tile([P, P], F32, name="perm")
-        bias_sb = keep.tile([P, 1024], F32, name="bias_sb")
+        bias_sb = keep.tile([P, 1024], BF16, name="bias_sb")
         w_codes = keep.tile([P, 2, 1024], U32, name="w_codes", align_bytes=64)
         w_scales = keep.tile([P, 2, 1024], U8, name="w_scales", align_bytes=64)
         w_grp = [[keep.tile([P, 512, 4], BF16, name="w_grp%d%d" % (g, h), align_bytes=64) for h in range(2)] for g in range(2)]
@@ -57,21 +57,21 @@ def tile_reasoningmultiheadattention_pb_kernel(tc, h_attn, Wo, bo, out):
         res = [keep.tile([P, 1024], F32, name="res%d" % m) for m in range(8)]
         banks = {}
 
+        nc.vector.memset(brow[:], 0.0)
+        nc.vector.memset(ones[:], 1.0)
         nc.sync.dma_start(out=w_raw[0][:], in_=w_view[0])
+        nc.sync.dma_start(out=brow[0:1, :], in_=bo.rearrange("(o n) -> o n", o=1))
         nc.sync.dma_start(out=x_raw[0][:], in_=h_flat[:, :, 0:512])
-        nc.sync.dma_start(out=w_raw[1][:], in_=w_view[1])
+        nc.sync.dma_start(out=w_raw[1][:, :, 0:512], in_=w_view[1][:, :, 0:512])
+        nc.sync.dma_start(out=w_raw[1][:, :, 512:1024], in_=w_view[1][:, :, 512:1024])
         nc.sync.dma_start(out=x_raw[1][:], in_=h_flat[:, :, 512:1024])
+
 
         def copy_on(engine, dst, src):
             if engine == "V":
                 nc.vector.tensor_copy(out=dst, in_=src)
             else:
                 nc.scalar.copy(out=dst, in_=src)
-
-        def op_ms():
-            nc.vector.memset(brow[:], 0.0)
-            nc.vector.memset(ones[:], 1.0)
-            nc.scalar.dma_start(out=brow[0:1, :], in_=bo.rearrange("(o n) -> o n", o=1))
 
         def op_ident():
             make_identity(nc, ident[:])
@@ -83,11 +83,13 @@ def tile_reasoningmultiheadattention_pb_kernel(tc, h_attn, Wo, bo, out):
             )
 
         def op_bm(h):
-            banks["b%d" % h] = psum.tile([P, 512], F32, name="bps%d" % h, tag="bank")
-            nc.tensor.matmul(out=banks["b%d" % h][:], lhsT=ones[:], rhs=brow[:, h * 512 : (h + 1) * 512], start=True, stop=True)
+            if h == 0:
+                banks["b"] = psum.tile([P, 1024], BF16, name="bps", tag="bank")
+            cols = slice(h * 512, (h + 1) * 512)
+            nc.tensor.matmul(out=banks["b"][:, cols], lhsT=ones[:], rhs=brow[:, cols], start=True, stop=True)
 
-        def op_bc(h):
-            nc.scalar.copy(out=bias_sb[:, h * 512 : (h + 1) * 512], in_=banks["b%d" % h][:])
+        def op_bc():
+            nc.scalar.copy(out=bias_sb[:], in_=banks["b"][:])
 
         def op_wi(engine, g, h):
             src = w_raw[g][:, :, h * 512 : (h + 1) * 512].rearrange("p j n -> p n j")
@@ -169,16 +171,14 @@ def tile_reasoningmultiheadattention_pb_kernel(tc, h_attn, Wo, bo, out):
 
         for name in ORDER.split():
             d = [int(ch) for ch in name if ch in "0123456789"]
-            if name == "ms":
-                op_ms()
-            elif name == "ident":
+            if name == "ident":
                 op_ident()
             elif name == "perm":
                 op_perm()
             elif name.startswith("bm"):
                 op_bm(d[0])
             elif name.startswith("bc"):
-                op_bc(d[0])
+                op_bc()
             elif name.startswith("wiV"):
                 op_wi("V", d[0], d[1])
             elif name.startswith("wiS"):

@@ -13,19 +13,15 @@ ADD = mybir.AluOpType.add
 FLOPS = 2 * 1024 * 1024 * 1024
 
 P = 128
-VS = [[336,336],[336,176]]
-RL_ENGINE = "VVSSSSSS"
-EV_ENGINE = "SSSSSSSS"
-MANUAL = True
-ORDER = """
-ident perm wiS00 wiV01 bm0 bm1 wiV00 wiS01 wq00 bc wq01 rl2 rl0 rl1 rl3 t0_0 t0_1 t0_2 t0_3 t1_0 t1_1 ev0 t1_2
-t1_3 t2_0 wiV10 t2_1 t2_2 t2_3 wiS10 t3_0 t3_1 t3_2 t3_3 yq0 ev1 wq10 mx000 ev2 yq1 mx001 wiV11 ev3 mx100
-mx101 yq2 wiS11 yq3 mx200 fa00 mx201 mx300 fa10 mx010 st00 mx301 fa20 rl4 mx110 st10 mx310 wq11 rl5 mx210 st20
-t4_0 t4_1 fa30 rl7 t4_2 t4_3 mx011 ev4 mx111 st30 fa01 mx211 yq4 t5_0 st01 t5_1 t5_2 t5_3 fa11 ev5 mx311 mx400
-fa31 st11 rl6 mx401 mx410 yq5 st31 mx411 fa40 t6_0 t6_1 t6_2 t6_3 fa21 st40 ev6 mx500 mx510 fa41 st21 mx501
-mx511 yq6 st41 t7_0 fa50 t7_1 t7_2 t7_3 ev7 mx600 fa51 st50 mx601 mx610 yq7 st51 mx611 fa60 mx700 mx710 fa61
-mx711 st60 mx701 st61 fa70 fa71 st70 st71
-"""
+PACK = 4
+PASSES = 2
+HALVES = 2
+HALF = 512
+ROW_TILES = 8
+CHUNK_TILES = 4
+
+VECTOR_COLUMNS = ((336, 336), (336, 176))
+REGROUPED_BY_VECTOR = (0, 1)
 
 
 def tile_reasoningmultiheadattention_pb_kernel(tc, h_attn, Wo, bo, out):
@@ -33,175 +29,175 @@ def tile_reasoningmultiheadattention_pb_kernel(tc, h_attn, Wo, bo, out):
     with ExitStack() as ctx:
         keep = ctx.enter_context(tc.tile_pool(name="keep", bufs=1))
         psum = ctx.enter_context(tc.psum_pool(name="psum", bufs=8))
-        if MANUAL:
-            ctx.enter_context(tc.manual_schedule())
+        ctx.enter_context(tc.manual_schedule())
 
-        h_flat = h_attn.rearrange("b (q j) h d -> (b q) j (h d)", j=8)
-        w_view = Wo.rearrange("(g p j) n -> g p j n", g=2, j=4)
+        h_view = h_attn.rearrange("b (q j) h d -> (b q) j (h d)", j=8)
+        w_view = Wo.rearrange("(g i t) n -> g i t n", g=PASSES, t=PACK)
         out_view = out.rearrange("b (m r) n -> m r b n", r=32)
 
-        brow = keep.tile([P, 1024], BF16, name="brow")
+        bias_row = keep.tile([P, 1024], BF16, name="bias_row")
         ones = keep.tile([P, P], BF16, name="ones")
-        w_raw = [keep.tile([P, 4, 1024], BF16, name="w_raw%d" % g) for g in range(2)]
-        x_raw = [keep.tile([P, 8, 512], BF16, name="x_raw%d" % c) for c in range(2)]
-        ident = keep.tile([P, P], F32, name="ident")
-        perm = keep.tile([P, P], F32, name="perm")
-        bias_sb = keep.tile([P, 1024], BF16, name="bias_sb")
-        w_codes = keep.tile([P, 2, 1024], U32, name="w_codes", align_bytes=64)
-        w_scales = keep.tile([P, 2, 1024], U8, name="w_scales", align_bytes=64)
-        w_grp = [[keep.tile([P, 512, 4], BF16, name="w_grp%d%d" % (g, h), align_bytes=64) for h in range(2)] for g in range(2)]
-        z = [keep.tile([P, 8, 2, P], F32, name="z%d" % c) for c in range(2)]
-        y_codes = [keep.tile([P, 256], U32, name="y_codes%d" % m, align_bytes=64) for m in range(8)]
-        y_scales = [keep.tile([P, 256], U8, name="y_scales%d" % m, align_bytes=64) for m in range(8)]
-        y_grp = [keep.tile([P, 1024], BF16, name="y_grp%d" % m, align_bytes=64) for m in range(8)]
-        res = [keep.tile([P, 1024], F32, name="res%d" % m) for m in range(8)]
-        banks = {}
+        bias = keep.tile([P, 1024], BF16, name="bias")
+        identity = keep.tile([P, P], F32, name="identity")
+        sorter = keep.tile([P, P], F32, name="sorter")
+        w_raw = [keep.tile([P, PACK, 1024], BF16, name="w_raw%d" % g) for g in range(PASSES)]
+        w_grouped = [
+            [keep.tile([P, HALF, PACK], BF16, name="w_grouped%d%d" % (g, h), align_bytes=64) for h in range(HALVES)]
+            for g in range(PASSES)
+        ]
+        w_codes = keep.tile([P, PASSES, 1024], U32, name="w_codes", align_bytes=64)
+        w_scales = keep.tile([P, PASSES, 1024], U8, name="w_scales", align_bytes=64)
+        y_raw = [keep.tile([P, 8, HALF], BF16, name="y_raw%d" % c) for c in range(2)]
+        y_sorted = [keep.tile([P, 8, 2, P], F32, name="y_sorted%d" % c) for c in range(2)]
+        y_grouped = [keep.tile([P, PASSES * P * PACK], BF16, name="y_grouped%d" % m, align_bytes=64) for m in range(ROW_TILES)]
+        y_codes = [keep.tile([P, PASSES * P], U32, name="y_codes%d" % m, align_bytes=64) for m in range(ROW_TILES)]
+        y_scales = [keep.tile([P, PASSES * P], U8, name="y_scales%d" % m, align_bytes=64) for m in range(ROW_TILES)]
+        res = [keep.tile([P, 1024], F32, name="res%d" % m) for m in range(ROW_TILES)]
+        turned = {}
+        acc = {}
 
-        nc.vector.memset(brow[:], 0.0)
-        nc.vector.memset(ones[:], 1.0)
-        nc.sync.dma_start(out=w_raw[0][:], in_=w_view[0])
-        nc.sync.dma_start(out=brow[0:1, :], in_=bo.rearrange("(o n) -> o n", o=1))
-        nc.sync.dma_start(out=x_raw[0][:], in_=h_flat[:, :, 0:512])
-        nc.sync.dma_start(out=w_raw[1][:, :, 0:512], in_=w_view[1][:, :, 0:512])
-        nc.sync.dma_start(out=w_raw[1][:, :, 512:1024], in_=w_view[1][:, :, 512:1024])
-        nc.sync.dma_start(out=x_raw[1][:], in_=h_flat[:, :, 512:1024])
+        def half_columns(h):
+            return slice(h * HALF, (h + 1) * HALF)
 
-
-        def copy_on(engine, dst, src):
-            if engine == "V":
+        def copy_on(vector, dst, src):
+            if vector:
                 nc.vector.tensor_copy(out=dst, in_=src)
             else:
                 nc.scalar.copy(out=dst, in_=src)
 
-        def op_ident():
-            make_identity(nc, ident[:])
+        def w_interleave(g, h):
+            src = w_raw[g][:, :, half_columns(h)].rearrange("i t n -> i n t")
+            cut = VECTOR_COLUMNS[g][h]
+            copy_on(True, w_grouped[g][h][:, 0:cut, :], src[:, 0:cut, :])
+            copy_on(False, w_grouped[g][h][:, cut:HALF, :], src[:, cut:HALF, :])
 
-        def op_perm():
-            nc.vector.tensor_copy(
-                out=perm[:].rearrange("p (g t b) -> p g t b", g=2, t=16, b=4),
-                in_=ident[:].rearrange("p (b t g) -> p g t b", b=4, t=16, g=2),
-            )
-
-        def op_bm(h):
-            if h == 0:
-                banks["b"] = psum.tile([P, 1024], BF16, name="bps", tag="bank")
-            cols = slice(h * 512, (h + 1) * 512)
-            nc.tensor.matmul(out=banks["b"][:, cols], lhsT=ones[:], rhs=brow[:, cols], start=True, stop=True)
-
-        def op_bc():
-            nc.scalar.copy(out=bias_sb[:], in_=banks["b"][:])
-
-        def op_wi(engine, g, h):
-            src = w_raw[g][:, :, h * 512 : (h + 1) * 512].rearrange("p j n -> p n j")
-            cut = VS[g][h]
-            if engine == "V":
-                copy_on("V", w_grp[g][h][:, 0:cut, :], src[:, 0:cut, :])
-            else:
-                copy_on("S", w_grp[g][h][:, cut:512, :], src[:, cut:512, :])
-
-        def op_wq(g, h):
-            cols = slice(h * 512, (h + 1) * 512)
+        def w_quantize(g, h):
             nc.vector.quantize_mx(
-                out=w_codes[:, g, cols].bitcast(E5M2X4),
-                scales=w_scales[:, g, cols],
-                in_=w_grp[g][h][:].rearrange("p n j -> p (n j)"),
+                out=w_codes[:, g, half_columns(h)].bitcast(E5M2X4),
+                scales=w_scales[:, g, half_columns(h)],
+                in_=w_grouped[g][h][:].rearrange("i n t -> i (n t)"),
             )
 
-        def op_rl(m):
-            c, l = divmod(m, 4)
-            xw = x_raw[c][:].rearrange("p j e -> p (j e)").bitcast(F32)
-            xw = xw.rearrange("p (j h q u) -> p h u j q", j=8, h=8, q=16, u=2)
+        def bias_broadcast():
+            bank = psum.tile([P, 1024], BF16, name="bias_bank", tag="bank")
+            for h in range(HALVES):
+                nc.tensor.matmul(
+                    out=bank[:, half_columns(h)], lhsT=ones[:], rhs=bias_row[:, half_columns(h)], start=True, stop=True
+                )
+            nc.scalar.copy(out=bias[:], in_=bank[:])
+
+        def y_regroup(m):
+            c, first = m // CHUNK_TILES, 2 * (m % CHUNK_TILES)
+            words = y_raw[c][:].rearrange("p j e -> p (j e)").bitcast(F32)
+            words = words.rearrange("p (j h q u) -> p h u j q", j=8, h=8, q=16, u=2)
             copy_on(
-                RL_ENGINE[m],
-                z[c][:, 2 * l : 2 * l + 2, :, :].rearrange("p h u (j q) -> p h u j q", j=8),
-                xw[:, 2 * l : 2 * l + 2, :, :, :],
+                m in REGROUPED_BY_VECTOR,
+                y_sorted[c][:, first : first + 2, :, :].rearrange("p h u (j q) -> p h u j q", j=8),
+                words[:, first : first + 2, :, :, :],
             )
 
-        def op_t(m, i):
-            c, l = divmod(m, 4)
-            a, u = divmod(i, 2)
-            if i == 0:
-                banks["t%d" % m] = psum.tile([P, 2, 2, 2, 64], F32, name="tp%d" % m, tag="bank")
-            nc.tensor.transpose(
-                banks["t%d" % m][:, :, u, a, :],
-                z[c][:, 2 * l + a, u, :],
-                perm[:].rearrange("p (g c) -> p g c", g=2),
+        def y_transpose(m):
+            c, first = m // CHUNK_TILES, 2 * (m % CHUNK_TILES)
+            turned[m] = psum.tile([P, PASSES, 2, 2, 64], F32, name="turned%d" % m, tag="bank")
+            for a in range(2):
+                for u in range(2):
+                    nc.tensor.transpose(
+                        turned[m][:, :, u, a, :],
+                        y_sorted[c][:, first + a, u, :],
+                        sorter[:].rearrange("p (g c) -> p g c", g=PASSES),
+                    )
+
+        def y_evacuate(m):
+            nc.scalar.copy(
+                out=y_grouped[m][:].bitcast(F32).rearrange("i (g c u) -> i g c u", g=PASSES, c=P, u=2),
+                in_=turned[m][:].rearrange("i g u a c -> i g (a c) u"),
             )
 
-        def op_ev(m):
-            copy_on(
-                EV_ENGINE[m],
-                y_grp[m][:].bitcast(F32).rearrange("p (g c u) -> p g c u", g=2, c=P, u=2),
-                banks["t%d" % m][:].rearrange("p g u a c -> p g (a c) u"),
-            )
+        def y_quantize(m):
+            nc.vector.quantize_mx(out=y_codes[m][:].bitcast(E5M2X4), scales=y_scales[m][:], in_=y_grouped[m][:])
 
-        def op_yq(m):
-            nc.vector.quantize_mx(out=y_codes[m][:].bitcast(E5M2X4), scales=y_scales[m][:], in_=y_grp[m][:])
-
-        def op_mx(m, h, g):
+        def mx_pass(m, h, g):
             if g == 0:
-                banks["a%d%d" % (m, h)] = psum.tile([P, 512], F32, name="acc%d%d" % (m, h), tag="bank")
-            cols = slice(h * 512, (h + 1) * 512)
+                acc[(m, h)] = psum.tile([P, HALF], F32, name="acc%d%d" % (m, h), tag="bank")
             rows = slice(g * P, (g + 1) * P)
             nc.tensor.matmul_mx(
-                out=banks["a%d%d" % (m, h)][:],
+                out=acc[(m, h)][:],
                 lhsT=y_codes[m][:, rows].bitcast(E5M2X4),
                 lhsT_scale=y_scales[m][:, rows],
-                rhs=w_codes[:, g, cols].bitcast(E5M2X4),
-                rhs_scale=w_scales[:, g, cols],
+                rhs=w_codes[:, g, half_columns(h)].bitcast(E5M2X4),
+                rhs_scale=w_scales[:, g, half_columns(h)],
                 start=(g == 0),
-                stop=(g == 1),
+                stop=(g == PASSES - 1),
             )
 
-        def op_fa(m, h):
-            cols = slice(h * 512, (h + 1) * 512)
-            nc.vector.tensor_tensor(out=res[m][:, cols], in0=banks["a%d%d" % (m, h)][:], in1=bias_sb[:, cols], op=ADD)
-
-        def op_fe(m, h):
-            cols = slice(h * 512, (h + 1) * 512)
-            nc.scalar.copy(out=res[m][:, cols], in_=banks["a%d%d" % (m, h)][:])
-
-        def op_fg(m, h):
-            cols = slice(h * 512, (h + 1) * 512)
-            nc.gpsimd.tensor_tensor(out=res[m][:, cols], in0=res[m][:, cols], in1=bias_sb[:, cols], op=ADD)
-
-        def op_st(m, h):
-            cols = slice(h * 512, (h + 1) * 512)
+        def finish(m, h):
+            cols = half_columns(h)
+            nc.vector.tensor_tensor(out=res[m][:, cols], in0=acc[(m, h)][:], in1=bias[:, cols], op=ADD)
             nc.sync.dma_start(out=out_view[m][:, :, cols], in_=res[m][:, cols])
 
-        for name in ORDER.split():
-            d = [int(ch) for ch in name if ch in "0123456789"]
-            if name == "ident":
-                op_ident()
-            elif name == "perm":
-                op_perm()
-            elif name.startswith("bm"):
-                op_bm(d[0])
-            elif name.startswith("bc"):
-                op_bc()
-            elif name.startswith("wiV"):
-                op_wi("V", d[0], d[1])
-            elif name.startswith("wiS"):
-                op_wi("S", d[0], d[1])
-            elif name.startswith("wq"):
-                op_wq(d[0], d[1])
-            elif name.startswith("rl"):
-                op_rl(d[0])
-            elif name.startswith("t"):
-                op_t(d[0], d[1])
-            elif name.startswith("ev"):
-                op_ev(d[0])
-            elif name.startswith("yq"):
-                op_yq(d[0])
-            elif name.startswith("mx"):
-                op_mx(d[0], d[1], d[2])
-            elif name.startswith("fa"):
-                op_fa(d[0], d[1])
-            elif name.startswith("fe"):
-                op_fe(d[0], d[1])
-            elif name.startswith("fg"):
-                op_fg(d[0], d[1])
-            elif name.startswith("st"):
-                op_st(d[0], d[1])
-            else:
-                assert False, name
+        nc.vector.memset(bias_row[:], 0.0)
+        nc.vector.memset(ones[:], 1.0)
+        nc.sync.dma_start(out=w_raw[0][:], in_=w_view[0])
+        nc.sync.dma_start(out=bias_row[0:1, :], in_=bo.rearrange("(o n) -> o n", o=1))
+        nc.sync.dma_start(out=y_raw[0][:], in_=h_view[:, :, half_columns(0)])
+        for h in range(HALVES):
+            nc.sync.dma_start(out=w_raw[1][:, :, half_columns(h)], in_=w_view[1][:, :, half_columns(h)])
+        nc.sync.dma_start(out=y_raw[1][:], in_=h_view[:, :, half_columns(1)])
+
+        make_identity(nc, identity[:])
+        nc.vector.tensor_copy(
+            out=sorter[:].rearrange("p (g t b) -> p g t b", g=2, t=16, b=4),
+            in_=identity[:].rearrange("p (b t g) -> p g t b", b=4, t=16, g=2),
+        )
+
+        for h in range(HALVES):
+            w_interleave(0, h)
+        bias_broadcast()
+        for h in range(HALVES):
+            w_quantize(0, h)
+
+        for m in range(CHUNK_TILES):
+            y_regroup(m)
+        for m in range(CHUNK_TILES):
+            y_transpose(m)
+        y_evacuate(0)
+        w_interleave(1, 0)
+        y_quantize(0)
+        w_quantize(1, 0)
+        y_evacuate(1)
+        y_quantize(1)
+        y_evacuate(2)
+        y_evacuate(3)
+        w_interleave(1, 1)
+        y_quantize(2)
+        y_quantize(3)
+        for m in range(CHUNK_TILES):
+            mx_pass(m, 0, 0)
+            mx_pass(m, 0, 1)
+            mx_pass(m, 1, 0)
+        for m in range(CHUNK_TILES - 1):
+            finish(m, 0)
+        w_quantize(1, 1)
+        finish(CHUNK_TILES - 1, 0)
+
+        y_regroup(CHUNK_TILES)
+        y_transpose(CHUNK_TILES)
+        for m in range(CHUNK_TILES):
+            mx_pass(m, 1, 1)
+        bank_pairs = [((0, 1), (1, 1)), ((2, 1), (3, 1))] + [((m, 0), (m, 1)) for m in range(CHUNK_TILES, ROW_TILES)]
+        for step, pair in enumerate(bank_pairs):
+            m = CHUNK_TILES + step
+            if m + 1 < ROW_TILES:
+                y_regroup(m + 1)
+            if m < ROW_TILES:
+                y_evacuate(m)
+            for bank in pair:
+                finish(bank[0], bank[1])
+            if m < ROW_TILES:
+                y_quantize(m)
+            if m + 1 < ROW_TILES:
+                y_transpose(m + 1)
+            if m < ROW_TILES:
+                for h in range(HALVES):
+                    for g in range(PASSES):
+                        mx_pass(m, h, g)

@@ -66,10 +66,11 @@ def tile_reasoningmultiheadattention_pb_kernel(tc, h_attn, Wo, bo, out):
                 nc.scalar.copy(out=dst, in_=src)
 
         def w_interleave(g, h):
-            src = w_raw[g][:, :, half_columns(h)].rearrange("i t n -> i n t")
-            cut = VECTOR_COLUMNS[g][h]
-            copy_on(True, w_grouped[g][h][:, 0:cut, :], src[:, 0:cut, :])
-            copy_on(False, w_grouped[g][h][:, cut:HALF, :], src[:, cut:HALF, :])
+            src = w_raw[g][:, :, half_columns(h)].rearrange("i t (c s) -> i c t s", s=4)
+            dst = w_grouped[g][h][:].rearrange("i (c s) t -> i c t s", s=4)
+            cut = VECTOR_COLUMNS[g][h] // 4
+            copy_on(True, dst[:, 0:cut, :, :], src[:, 0:cut, :, :])
+            copy_on(False, dst[:, cut : HALF // 4, :, :], src[:, cut : HALF // 4, :, :])
 
         def w_quantize(g, h):
             nc.vector.quantize_mx(

@@ -55,6 +55,7 @@ def tile_reasoningmultiheadattention_pb_kernel(tc, h_attn, Wo, bo, out):
         res = [keep.tile([P, 1024], F32, name="res%d" % m) for m in range(ROW_TILES)]
         turned = {}
         acc = {}
+        idle_bank = psum.tile([P, HALF], F32, name="idle_bank", tag="bank")
 
         def half_columns(h):
             return slice(h * HALF, (h + 1) * HALF)
@@ -66,11 +67,20 @@ def tile_reasoningmultiheadattention_pb_kernel(tc, h_attn, Wo, bo, out):
                 nc.scalar.copy(out=dst, in_=src)
 
         def w_interleave(g, h):
-            src = w_raw[g][:, :, half_columns(h)].rearrange("i t (c s) -> i c t s", s=4)
-            dst = w_grouped[g][h][:].rearrange("i (c s) t -> i c t s", s=4)
-            cut = VECTOR_COLUMNS[g][h] // 4
-            copy_on(True, dst[:, 0:cut, :, :], src[:, 0:cut, :, :])
-            copy_on(False, dst[:, cut : HALF // 4, :, :], src[:, cut : HALF // 4, :, :])
+            src = w_raw[g][:, :, half_columns(h)].rearrange("i t n -> i n t")
+            cut = VECTOR_COLUMNS[g][h]
+            copy_on(True, w_grouped[g][h][:, 0:cut, :], src[:, 0:cut, :])
+            copy_on(False, w_grouped[g][h][:, cut:HALF, :], src[:, cut:HALF, :])
+
+        def keep_busy(h):
+            for repeat in range(2):
+                nc.tensor.matmul(
+                    out=idle_bank[:],
+                    lhsT=ones[:],
+                    rhs=w_grouped[0][h][:, 0:P, :].rearrange("i n t -> i (n t)"),
+                    start=True,
+                    stop=True,
+                )
 
         def w_quantize(g, h):
             nc.vector.quantize_mx(
@@ -155,12 +165,16 @@ def tile_reasoningmultiheadattention_pb_kernel(tc, h_attn, Wo, bo, out):
             w_interleave(0, h)
         bias_broadcast()
         for h in range(HALVES):
+            keep_busy(h)
+        for h in range(HALVES):
             w_quantize(0, h)
 
         for m in range(CHUNK_TILES):
             y_regroup(m)
         for m in range(CHUNK_TILES):
             y_transpose(m)
+            if m % 2 == 1:
+                keep_busy(1)
         y_evacuate(0)
         w_interleave(1, 0)
         y_quantize(0)

@@ -22,6 +22,7 @@ CHUNK_TILES = 4
 
 VECTOR_COLUMNS = ((336, 336), (336, 176))
 REGROUPED_BY_VECTOR = (0, 1)
+BESIDE_VECTOR = (1, 1)
 
 
 def tile_reasoningmultiheadattention_pb_kernel(tc, h_attn, Wo, bo, out):
@@ -53,6 +54,7 @@ def tile_reasoningmultiheadattention_pb_kernel(tc, h_attn, Wo, bo, out):
         y_codes = [keep.tile([P, PASSES * P], U32, name="y_codes%d" % m, align_bytes=64) for m in range(ROW_TILES)]
         y_scales = [keep.tile([P, PASSES * P], U8, name="y_scales%d" % m, align_bytes=64) for m in range(ROW_TILES)]
         res = [keep.tile([P, 1024], F32, name="res%d" % m) for m in range(ROW_TILES)]
+        product = keep.tile([P, HALF], F32, name="product")
         turned = {}
         acc = {}
         idle_bank = psum.tile([P, HALF], F32, name="idle_bank", tag="bank")
@@ -146,6 +148,13 @@ def tile_reasoningmultiheadattention_pb_kernel(tc, h_attn, Wo, bo, out):
             nc.vector.tensor_tensor(out=res[m][:, cols], in0=acc[(m, h)][:], in1=bias[:, cols], op=ADD)
             nc.sync.dma_start(out=out_view[m][:, :, cols], in_=res[m][:, cols])
 
+        def finish_beside_vector(m, h):
+            nc.scalar.copy(out=product[:], in_=acc[(m, h)][:])
+            nc.gpsimd.tensor_tensor(out=res[m][:, half_columns(h)], in0=product[:], in1=bias[:, half_columns(h)], op=ADD)
+
+        def store_beside_vector(m, h):
+            nc.scalar.dma_start(out=out_view[m][:, :, half_columns(h)], in_=res[m][:, half_columns(h)])
+
         nc.vector.memset(bias_row[:], 0.0)
         nc.vector.memset(ones[:], 1.0)
         nc.sync.dma_start(out=w_raw[0][:], in_=w_view[0])
@@ -206,8 +215,13 @@ def tile_reasoningmultiheadattention_pb_kernel(tc, h_attn, Wo, bo, out):
                 y_regroup(m + 1)
             if m < ROW_TILES:
                 y_evacuate(m)
+            if BESIDE_VECTOR in bank_pairs[step - 1] and step > 0:
+                store_beside_vector(BESIDE_VECTOR[0], BESIDE_VECTOR[1])
             for bank in pair:
-                finish(bank[0], bank[1])
+                if bank == BESIDE_VECTOR:
+                    finish_beside_vector(bank[0], bank[1])
+                else:
+                    finish(bank[0], bank[1])
             if m < ROW_TILES:
                 y_quantize(m)
             if m + 1 < ROW_TILES:

@@ -175,11 +175,11 @@ def tile_reasoningmultiheadattention_pb_kernel(tc, h_attn, Wo, bo, out):
         bias_broadcast()
         for h in range(HALVES):
             keep_busy(h)
-        for h in range(HALVES):
-            w_quantize(0, h)
+        w_quantize(0, 0)
 
         for m in range(CHUNK_TILES):
             y_regroup(m)
+        w_quantize(0, 1)
         for m in range(CHUNK_TILES):
             y_transpose(m)
             if m % 2 == 1:
@@ -199,10 +199,11 @@ def tile_reasoningmultiheadattention_pb_kernel(tc, h_attn, Wo, bo, out):
             mx_pass(m, 0, 0)
             mx_pass(m, 0, 1)
             mx_pass(m, 1, 0)
-        for m in range(CHUNK_TILES - 1):
+        for m in range(2):
             finish(m, 0)
         w_quantize(1, 1)
-        finish(CHUNK_TILES - 1, 0)
+        for m in range(2, CHUNK_TILES):
+            finish(m, 0)
 
         y_regroup(CHUNK_TILES)
         y_transpose(CHUNK_TILES)

@@ -99,14 +99,14 @@ def tile_reasoningmultiheadattention_pb_kernel(tc, h_attn, Wo, bo, out):
                 )
             nc.scalar.copy(out=bias[:], in_=bank[:])
 
-        def y_regroup(m):
+        def y_regroup(m, tiles=1):
             c, first = m // CHUNK_TILES, 2 * (m % CHUNK_TILES)
             words = y_raw[c][:].rearrange("p j e -> p (j e)").bitcast(F32)
             words = words.rearrange("p (j h q u) -> p h u j q", j=8, h=8, q=16, u=2)
             copy_on(
                 m in REGROUPED_BY_VECTOR,
-                y_sorted[c][:, first : first + 2, :, :].rearrange("p h u (j q) -> p h u j q", j=8),
-                words[:, first : first + 2, :, :, :],
+                y_sorted[c][:, first : first + 2 * tiles, :, :].rearrange("p h u (j q) -> p h u j q", j=8),
+                words[:, first : first + 2 * tiles, :, :, :],
             )
 
         def y_transpose(m):
@@ -143,10 +143,14 @@ def tile_reasoningmultiheadattention_pb_kernel(tc, h_attn, Wo, bo, out):
                 stop=(g == PASSES - 1),
             )
 
-        def finish(m, h):
-            cols = half_columns(h)
-            nc.vector.tensor_tensor(out=res[m][:, cols], in0=acc[(m, h)][:], in1=bias[:, cols], op=ADD)
-            nc.sync.dma_start(out=out_view[m][:, :, cols], in_=res[m][:, cols])
+        def finish(m, h, pieces=1):
+            width = HALF // pieces
+            for piece in range(pieces):
+                cols = slice(h * HALF + piece * width, h * HALF + (piece + 1) * width)
+                nc.vector.tensor_tensor(
+                    out=res[m][:, cols], in0=acc[(m, h)][:, piece * width : (piece + 1) * width], in1=bias[:, cols], op=ADD
+                )
+                nc.sync.dma_start(out=out_view[m][:, :, cols], in_=res[m][:, cols])
 
         def finish_beside_vector(m, h):
             nc.scalar.copy(out=product[:], in_=acc[(m, h)][:])
@@ -177,8 +181,9 @@ def tile_reasoningmultiheadattention_pb_kernel(tc, h_attn, Wo, bo, out):
             keep_busy(h)
         w_quantize(0, 0)
 
-        for m in range(CHUNK_TILES):
-            y_regroup(m)
+        y_regroup(0)
+        y_regroup(1)
+        y_regroup(2, tiles=2)
         w_quantize(0, 1)
         for m in range(CHUNK_TILES):
             y_transpose(m)
@@ -222,7 +227,7 @@ def tile_reasoningmultiheadattention_pb_kernel(tc, h_attn, Wo, bo, out):
                 if bank == BESIDE_VECTOR:
                     finish_beside_vector(bank[0], bank[1])
                 else:
-                    finish(bank[0], bank[1])
+                    finish(bank[0], bank[1], pieces=2 if bank == (ROW_TILES - 1, HALVES - 1) else 1)
             if m < ROW_TILES:
                 y_quantize(m)
             if m + 1 < ROW_TILES:

@@ -20,7 +20,7 @@ HALF = 512
 ROW_TILES = 8
 CHUNK_TILES = 4
 
-VECTOR_COLUMNS = ((336, 336), (336, 176))
+VECTOR_COLUMNS = ((336, 336), (384, 176))
 REGROUPED_BY_VECTOR = (0, 1)
 BESIDE_VECTOR = (1, 1)
 

@@ -153,8 +153,12 @@ def tile_reasoningmultiheadattention_pb_kernel(tc, h_attn, Wo, bo, out):
                 nc.sync.dma_start(out=out_view[m][:, :, cols], in_=res[m][:, cols])
 
         def finish_beside_vector(m, h):
-            nc.scalar.copy(out=product[:], in_=acc[(m, h)][:])
-            nc.gpsimd.tensor_tensor(out=res[m][:, half_columns(h)], in0=product[:], in1=bias[:, half_columns(h)], op=ADD)
+            width = HALF // 2
+            for piece in range(2):
+                part = slice(piece * width, (piece + 1) * width)
+                cols = slice(h * HALF + piece * width, h * HALF + (piece + 1) * width)
+                nc.scalar.copy(out=product[:, part], in_=acc[(m, h)][:, part])
+                nc.gpsimd.tensor_tensor(out=res[m][:, cols], in0=product[:, part], in1=bias[:, cols], op=ADD)
 
         def store_beside_vector(m, h):
             nc.scalar.dma_start(out=out_view[m][:, :, half_columns(h)], in_=res[m][:, half_columns(h)])

from contextlib import ExitStack

import concourse.mybir as mybir
from concourse.masks import make_identity

F32 = mybir.dt.float32
BF16 = mybir.dt.bfloat16
U32 = mybir.dt.uint32
U8 = mybir.dt.uint8
E5M2X4 = mybir.dt.float8_e5m2_x4
ADD = mybir.AluOpType.add

FLOPS = 2 * 1024 * 1024 * 1024

P = 128
PACK = 4
PASSES = 2
HALVES = 2
HALF = 512
ROW_TILES = 8
CHUNK_TILES = 4

VECTOR_COLUMNS = ((336, 336), (384, 176))
REGROUPED_BY_VECTOR = (0, 1)
BESIDE_VECTOR = (1, 1)


def tile_reasoningmultiheadattention_pb_kernel(tc, h_attn, Wo, bo, out):
    nc = tc.nc
    with ExitStack() as ctx:
        keep = ctx.enter_context(tc.tile_pool(name="keep", bufs=1))
        psum = ctx.enter_context(tc.psum_pool(name="psum", bufs=8))
        ctx.enter_context(tc.manual_schedule())

        h_view = h_attn.rearrange("b (q j) h d -> (b q) j (h d)", j=8)
        w_view = Wo.rearrange("(g i t) n -> g i t n", g=PASSES, t=PACK)
        out_view = out.rearrange("b (m r) n -> m r b n", r=32)

        bias_row = keep.tile([P, 1024], BF16, name="bias_row")
        ones = keep.tile([P, P], BF16, name="ones")
        bias = keep.tile([P, 1024], BF16, name="bias")
        identity = keep.tile([P, P], F32, name="identity")
        sorter = keep.tile([P, P], F32, name="sorter")
        w_raw = [keep.tile([P, PACK, 1024], BF16, name="w_raw%d" % g) for g in range(PASSES)]
        w_grouped = [
            [keep.tile([P, HALF, PACK], BF16, name="w_grouped%d%d" % (g, h), align_bytes=64) for h in range(HALVES)]
            for g in range(PASSES)
        ]
        w_codes = keep.tile([P, PASSES, 1024], U32, name="w_codes", align_bytes=64)
        w_scales = keep.tile([P, PASSES, 1024], U8, name="w_scales", align_bytes=64)
        y_raw = [keep.tile([P, 8, HALF], BF16, name="y_raw%d" % c) for c in range(2)]
        y_sorted = [keep.tile([P, 8, 2, P], F32, name="y_sorted%d" % c) for c in range(2)]
        y_grouped = [keep.tile([P, PASSES * P * PACK], BF16, name="y_grouped%d" % m, align_bytes=64) for m in range(ROW_TILES)]
        y_codes = [keep.tile([P, PASSES * P], U32, name="y_codes%d" % m, align_bytes=64) for m in range(ROW_TILES)]
        y_scales = [keep.tile([P, PASSES * P], U8, name="y_scales%d" % m, align_bytes=64) for m in range(ROW_TILES)]
        res = [keep.tile([P, 1024], F32, name="res%d" % m) for m in range(ROW_TILES)]
        product = keep.tile([P, HALF], F32, name="product")
        turned = {}
        acc = {}
        idle_bank = psum.tile([P, HALF], F32, name="idle_bank", tag="bank")

        def half_columns(h):
            return slice(h * HALF, (h + 1) * HALF)

        def copy_on(vector, dst, src):
            if vector:
                nc.vector.tensor_copy(out=dst, in_=src)
            else:
                nc.scalar.copy(out=dst, in_=src)

        def w_interleave(g, h):
            src = w_raw[g][:, :, half_columns(h)].rearrange("i t n -> i n t")
            cut = VECTOR_COLUMNS[g][h]
            copy_on(True, w_grouped[g][h][:, 0:cut, :], src[:, 0:cut, :])
            copy_on(False, w_grouped[g][h][:, cut:HALF, :], src[:, cut:HALF, :])

        def keep_busy(h):
            for repeat in range(2):
                nc.tensor.matmul(
                    out=idle_bank[:],
                    lhsT=ones[:],
                    rhs=w_grouped[0][h][:, 0:P, :].rearrange("i n t -> i (n t)"),
                    start=True,
                    stop=True,
                )

        def w_quantize(g, h):
            nc.vector.quantize_mx(
                out=w_codes[:, g, half_columns(h)].bitcast(E5M2X4),
                scales=w_scales[:, g, half_columns(h)],
                in_=w_grouped[g][h][:].rearrange("i n t -> i (n t)"),
            )

        def bias_broadcast():
            bank = psum.tile([P, 1024], BF16, name="bias_bank", tag="bank")
            for h in range(HALVES):
                nc.tensor.matmul(
                    out=bank[:, half_columns(h)], lhsT=ones[:], rhs=bias_row[:, half_columns(h)], start=True, stop=True
                )
            nc.scalar.copy(out=bias[:], in_=bank[:])

        def y_regroup(m, tiles=1):
            c, first = m // CHUNK_TILES, 2 * (m % CHUNK_TILES)
            words = y_raw[c][:].rearrange("p j e -> p (j e)").bitcast(F32)
            words = words.rearrange("p (j h q u) -> p h u j q", j=8, h=8, q=16, u=2)
            copy_on(
                m in REGROUPED_BY_VECTOR,
                y_sorted[c][:, first : first + 2 * tiles, :, :].rearrange("p h u (j q) -> p h u j q", j=8),
                words[:, first : first + 2 * tiles, :, :, :],
            )

        def y_transpose(m):
            c, first = m // CHUNK_TILES, 2 * (m % CHUNK_TILES)
            turned[m] = psum.tile([P, PASSES, 2, 2, 64], F32, name="turned%d" % m, tag="bank")
            for a in range(2):
                for u in range(2):
                    nc.tensor.transpose(
                        turned[m][:, :, u, a, :],
                        y_sorted[c][:, first + a, u, :],
                        sorter[:].rearrange("p (g c) -> p g c", g=PASSES),
                    )

        def y_evacuate(m):
            nc.scalar.copy(
                out=y_grouped[m][:].bitcast(F32).rearrange("i (g c u) -> i g c u", g=PASSES, c=P, u=2),
                in_=turned[m][:].rearrange("i g u a c -> i g (a c) u"),
            )

        def y_quantize(m):
            nc.vector.quantize_mx(out=y_codes[m][:].bitcast(E5M2X4), scales=y_scales[m][:], in_=y_grouped[m][:])

        def mx_pass(m, h, g):
            if g == 0:
                acc[(m, h)] = psum.tile([P, HALF], F32, name="acc%d%d" % (m, h), tag="bank")
            rows = slice(g * P, (g + 1) * P)
            nc.tensor.matmul_mx(
                out=acc[(m, h)][:],
                lhsT=y_codes[m][:, rows].bitcast(E5M2X4),
                lhsT_scale=y_scales[m][:, rows],
                rhs=w_codes[:, g, half_columns(h)].bitcast(E5M2X4),
                rhs_scale=w_scales[:, g, half_columns(h)],
                start=(g == 0),
                stop=(g == PASSES - 1),
            )

        def finish(m, h, pieces=1):
            width = HALF // pieces
            for piece in range(pieces):
                cols = slice(h * HALF + piece * width, h * HALF + (piece + 1) * width)
                nc.vector.tensor_tensor(
                    out=res[m][:, cols], in0=acc[(m, h)][:, piece * width : (piece + 1) * width], in1=bias[:, cols], op=ADD
                )
                nc.sync.dma_start(out=out_view[m][:, :, cols], in_=res[m][:, cols])

        def finish_beside_vector(m, h):
            width = HALF // 2
            for piece in range(2):
                part = slice(piece * width, (piece + 1) * width)
                cols = slice(h * HALF + piece * width, h * HALF + (piece + 1) * width)
                nc.scalar.copy(out=product[:, part], in_=acc[(m, h)][:, part])
                nc.gpsimd.tensor_tensor(out=res[m][:, cols], in0=product[:, part], in1=bias[:, cols], op=ADD)

        def store_beside_vector(m, h):
            nc.scalar.dma_start(out=out_view[m][:, :, half_columns(h)], in_=res[m][:, half_columns(h)])

        nc.vector.memset(bias_row[:], 0.0)
        nc.vector.memset(ones[:], 1.0)
        nc.sync.dma_start(out=w_raw[0][:], in_=w_view[0])
        nc.sync.dma_start(out=bias_row[0:1, :], in_=bo.rearrange("(o n) -> o n", o=1))
        nc.sync.dma_start(out=y_raw[0][:], in_=h_view[:, :, half_columns(0)])
        for h in range(HALVES):
            nc.sync.dma_start(out=w_raw[1][:, :, half_columns(h)], in_=w_view[1][:, :, half_columns(h)])
        nc.sync.dma_start(out=y_raw[1][:], in_=h_view[:, :, half_columns(1)])

        make_identity(nc, identity[:])
        nc.vector.tensor_copy(
            out=sorter[:].rearrange("p (g t b) -> p g t b", g=2, t=16, b=4),
            in_=identity[:].rearrange("p (b t g) -> p g t b", b=4, t=16, g=2),
        )

        for h in range(HALVES):
            w_interleave(0, h)
        bias_broadcast()
        for h in range(HALVES):
            keep_busy(h)
        w_quantize(0, 0)

        y_regroup(0)
        y_regroup(1)
        y_regroup(2, tiles=2)
        w_quantize(0, 1)
        for m in range(CHUNK_TILES):
            y_transpose(m)
            if m % 2 == 1:
                keep_busy(1)
        y_evacuate(0)
        w_interleave(1, 0)
        y_quantize(0)
        w_quantize(1, 0)
        y_evacuate(1)
        y_quantize(1)
        y_evacuate(2)
        y_evacuate(3)
        w_interleave(1, 1)
        y_quantize(2)
        y_quantize(3)
        for m in range(CHUNK_TILES):
            mx_pass(m, 0, 0)
            mx_pass(m, 0, 1)
            mx_pass(m, 1, 0)
        for m in range(2):
            finish(m, 0)
        w_quantize(1, 1)
        for m in range(2, CHUNK_TILES):
            finish(m, 0)

        y_regroup(CHUNK_TILES)
        y_transpose(CHUNK_TILES)
        for m in range(CHUNK_TILES):
            mx_pass(m, 1, 1)
        bank_pairs = [((0, 1), (1, 1)), ((2, 1), (3, 1))] + [((m, 0), (m, 1)) for m in range(CHUNK_TILES, ROW_TILES)]
        for step, pair in enumerate(bank_pairs):
            m = CHUNK_TILES + step
            if m + 1 < ROW_TILES:
                y_regroup(m + 1)
            if m < ROW_TILES:
                y_evacuate(m)
            if BESIDE_VECTOR in bank_pairs[step - 1] and step > 0:
                store_beside_vector(BESIDE_VECTOR[0], BESIDE_VECTOR[1])
            for bank in pair:
                if bank == BESIDE_VECTOR:
                    finish_beside_vector(bank[0], bank[1])
                else:
                    finish(bank[0], bank[1], pieces=2 if bank == (ROW_TILES - 1, HALVES - 1) else 1)
            if m < ROW_TILES:
                y_quantize(m)
            if m + 1 < ROW_TILES:
                y_transpose(m + 1)
            if m < ROW_TILES:
                for h in range(HALVES):
                    for g in range(PASSES):
                        mx_pass(m, h, g)
